import numpy as np
import ml_dtypes


def mxq(x, axis, fmt="e4m3"):
    dtype, down = {"e4m3": (ml_dtypes.float8_e4m3fn, 7), "e5m2": (ml_dtypes.float8_e5m2, 14)}[fmt]
    v = np.moveaxis(np.asarray(x, np.float32).astype(ml_dtypes.bfloat16).astype(np.float64), axis, -1)
    blocks = v.reshape(v.shape[:-1] + (-1, 32))
    amax = np.abs(blocks).max(-1, keepdims=True)
    byte = np.maximum(np.where(amax > 0, np.frexp(amax)[1] - 1 + 127, 0) - down, 1)
    scale = np.exp2(byte - 127.0)
    codes = (blocks / scale).astype(np.float32).astype(dtype).astype(np.float64)
    return np.moveaxis((codes * scale).reshape(v.shape), -1, axis)


WIDE = False


def mx_kscale(k):
    if not WIDE:
        return np.ones(k)
    levels = np.array([10, -10, 5, -5, 0])
    a = np.random.permutation(np.resize(levels, k // 512 * 4)).reshape(k // 512, 4)
    idx = np.arange(k)
    return np.exp2(a[idx // 512, idx % 128 // 32])


BF16 = ml_dtypes.bfloat16


def bf(x):
    return np.asarray(x, np.float32).astype(BF16)


def f64(x):
    return np.asarray(x).astype(np.float64)


E2M1 = np.array([0.0, 0.5, 1.0, 1.5, 2.0, 3.0, 4.0, 6.0, -0.0, -0.5, -1.0, -1.5, -2.0, -3.0, -4.0, -6.0])


def pack_weight(w, fmt):
    k, n = w.shape
    w = f64(bf(w)).reshape(k // 32, 32, n)
    amax = np.abs(w).max(1)
    if fmt == "e4m3":
        byte = np.frexp(amax)[1] - 1 + 127 - 7
    else:
        mant, ex = np.frexp(amax / 6.0)
        byte = np.where(mant > 0.5, ex, ex - 1) + 127
    byte = np.clip(np.where(amax > 0, byte, 1), 1, 254)
    scaled = (w * np.exp2(127.0 - byte)[:, None, :]).reshape(k, n).astype(np.float32)
    by_word = np.ascontiguousarray(scaled.reshape(k // 512, 128, 4, n).transpose(0, 1, 3, 2))
    if fmt == "e4m3":
        words = by_word.astype(ml_dtypes.float8_e4m3fn).view(np.uint8)
    else:
        c = by_word.astype(ml_dtypes.float4_e2m1fn).view(np.uint8) & 0xF
        words = c[..., 0::2] | (c[..., 1::2] << 4)
    return np.ascontiguousarray(words), np.ascontiguousarray(byte.astype(np.uint8).reshape(k // 512, 16, n))


def unpack_weight(words, scales, fmt):
    g, p, n, _ = words.shape
    if fmt == "e4m3":
        vals = np.ascontiguousarray(words).view(ml_dtypes.float8_e4m3fn).astype(np.float64)
    else:
        nib = np.empty((g, p, n, 4), np.uint8)
        nib[..., 0::2] = words & 0xF
        nib[..., 1::2] = words >> 4
        vals = E2M1[nib]
    vals = vals * np.repeat(np.exp2(scales.astype(np.float64) - 127.0), 8, axis=1)[..., None]
    return vals.transpose(0, 1, 3, 2).reshape(g * 512, n)


B, C, CQ, H, W, D = 1, 1024, 128, 64, 64, 4
HP, WP = H // D, W // D
N = HP * WP
FMT = "e4m3"


def conv1x1(xq, w_words, w_scales, b):
    y = xq @ unpack_weight(w_words, w_scales, FMT)
    return y.transpose(0, 2, 1).reshape(B, -1, H, W) + f64(b)[None, :, None, None]


def maxpool(y):
    return y.reshape(B, -1, HP, D, WP, D).max(axis=(3, 5))


def setup_inputs():
    s = mx_kscale(C)
    x = bf(np.random.standard_normal((B, C, H, W)) * s[None, :, None, None])
    wq = np.random.standard_normal((CQ, C)) * 0.4 / np.sqrt(C) / s[None, :]
    bq = bf(np.random.standard_normal(CQ) * 0.1)
    wk = np.random.standard_normal((CQ, C)) * 0.4 / np.sqrt(C) / s[None, :]
    bk = bf(np.random.standard_normal(CQ) * 0.1)
    wv = np.random.standard_normal((C, C)) / np.sqrt(C) / s[None, :]
    bv = bf(np.random.standard_normal(C) * 0.1)
    wq_words, wq_scales = pack_weight(np.ascontiguousarray(wq.T), FMT)
    wk_words, wk_scales = pack_weight(np.ascontiguousarray(wk.T), FMT)
    wv_words, wv_scales = pack_weight(np.ascontiguousarray(wv.T), FMT)
    return {"x": x,
            "wq_words": wq_words, "wq_scales": wq_scales,
            "bq": bq,
            "wk_words": wk_words, "wk_scales": wk_scales,
            "bk": bk,
            "wv_words": wv_words, "wv_scales": wv_scales,
            "bv": bv}


def reference(x, wq_words, wq_scales, bq, wk_words, wk_scales, bk, wv_words, wv_scales, bv):
    xq = mxq(f64(x), 1, "e4m3").reshape(B, C, H * W).transpose(0, 2, 1)
    q = maxpool(conv1x1(xq, wq_words, wq_scales, bq)).reshape(B, -1, N).transpose(0, 2, 1)
    k = maxpool(conv1x1(xq, wk_words, wk_scales, bk)).reshape(B, -1, N)
    v = maxpool(conv1x1(xq, wv_words, wv_scales, bv)).reshape(B, C, N)
    return q, k, v

@@ -1,0 +1,189 @@
+from contextlib import ExitStack
+
+import concourse.mybir as mybir
+from concourse.masks import make_identity
+
+F32 = mybir.dt.float32
+BF16 = mybir.dt.bfloat16
+I32 = mybir.dt.int32
+U32 = mybir.dt.uint32
+U8 = mybir.dt.uint8
+FP8X4 = mybir.dt.float8_e4m3fn_x4
+
+P = 128
+PACK = 4
+CHANNELS = 1024
+PASSES = CHANNELS // (P * PACK)
+QUADRANTS = 4
+LIVE_ROWS = 4
+
+WIDTH = 64
+POOL = 4
+PIXELS = WIDTH * WIDTH
+CHUNK = 512
+CHUNKS = PIXELS // CHUNK
+POOLED_ROWS = CHUNK // (WIDTH * POOL)
+POOLED_COLS = WIDTH // POOL
+WINDOWS = POOLED_ROWS * POOLED_COLS
+POSITIONS = PIXELS // (POOL * POOL)
+
+V_OUT = 1024
+V_TILES = V_OUT // P
+Q_TILE = V_TILES
+K_TILE = V_TILES + 1
+O_TILES = V_TILES + 2
+O_ALL = O_TILES * P
+
+RUN = 4
+ACC_BANKS = 7
+STAGE_AT = 7
+
+FLOPS = 2 * O_ALL * CHANNELS * PIXELS
+
+
+def tile_selfattentionpatch_pa_t_kernel(
+    tc, x, wq_words, wq_scales, bq, wk_words, wk_scales, bk, wv_words, wv_scales, bv,
+    out_q, out_k, out_v,
+):
+    nc = tc.nc
+    with ExitStack() as ctx:
+        keep = ctx.enter_context(tc.tile_pool(name="keep", bufs=1))
+        raw_pool = ctx.enter_context(tc.tile_pool(name="raw", bufs=CHUNKS))
+        grouped_pool = ctx.enter_context(tc.tile_pool(name="grouped", bufs=3))
+        code_pool = ctx.enter_context(tc.tile_pool(name="codes", bufs=CHUNKS))
+        acc_pool = ctx.enter_context(tc.psum_pool(name="acc", bufs=ACC_BANKS))
+        flip_pool = ctx.enter_context(tc.psum_pool(name="flip", bufs=1))
+        ctx.enter_context(tc.manual_schedule())
+
+        w_words = keep.tile([P, PASSES, O_ALL], U32, align_bytes=64)
+        w_planes = keep.tile([P, PASSES, O_ALL], U8, align_bytes=64)
+        bias_rows = keep.tile([P, P], BF16)
+        bias_rows_f32 = keep.tile([P, P], F32)
+        bias_cols = keep.tile([P, O_TILES], F32)
+        identity = keep.tile([P, P], F32)
+        pooled = keep.tile([P, O_TILES, POSITIONS], F32)
+        result = keep.tile([P, O_TILES, POSITIONS], F32)
+        q_flipped = keep.tile([P, POSITIONS // P, P], F32)
+
+        nc.vector.memset(w_planes[:].rearrange("p g o -> p (g o)").bitcast(I32), 0)
+        nc.vector.memset(bias_rows[:].bitcast(I32), 0)
+        make_identity(nc, identity[:])
+
+        x_rows = x.rearrange("b (g p t) h w -> (b g) p t (h w)", p=P, t=PACK)
+        raw = []
+
+        def load_chunk(c):
+            raw.append(raw_pool.tile([P, PASSES, PACK, CHUNK], BF16, name="raw"))
+            for g in range(PASSES):
+                nc.sync.dma_start(
+                    out=raw[c][:, g], in_=x_rows[g, :, :, c * CHUNK : (c + 1) * CHUNK]
+                )
+
+        def load_scales(scales, first, count):
+            rows = scales.rearrange("g (q r) o -> q r g o", r=LIVE_ROWS)
+            for q in range(QUADRANTS):
+                nc.sync.dma_start(
+                    out=w_planes[32 * q : 32 * q + LIVE_ROWS, :, first : first + count].bitcast(I32),
+                    in_=rows[q].bitcast(I32),
+                )
+
+        def load_words(words, first, begin, end):
+            view = words.rearrange("g p o t -> p g (o t)")
+            nc.sync.dma_start(
+                out=w_words[:, :, first + begin : first + end].bitcast(I32),
+                in_=view[:, :, PACK * begin : PACK * end].bitcast(I32),
+            )
+
+        load_chunk(0)
+        load_scales(wv_scales, 0, V_OUT)
+        load_words(wv_words, 0, 0, V_OUT // 2)
+        load_words(wv_words, 0, V_OUT // 2, V_OUT)
+        nc.scalar.dma_start(out=bias_rows[0:V_TILES, :], in_=bv.rearrange("(r o) -> r o", o=P))
+        nc.scalar.dma_start(out=bias_rows[Q_TILE : Q_TILE + 1, :], in_=bq.rearrange("(r o) -> r o", o=P))
+        nc.scalar.dma_start(out=bias_rows[K_TILE : K_TILE + 1, :], in_=bk.rearrange("(r o) -> r o", o=P))
+        load_chunk(1)
+        load_scales(wq_scales, Q_TILE * P, P)
+        load_words(wq_words, Q_TILE * P, 0, P)
+        load_scales(wk_scales, K_TILE * P, P)
+        load_words(wk_words, K_TILE * P, 0, P)
+        for c in range(2, CHUNKS):
+            load_chunk(c)
+
+        x_codes = []
+        x_scales = []
+
+        def stage_chunk(c, copy):
+            grouped = grouped_pool.tile([P, PASSES, CHUNK, PACK], BF16, align_bytes=64)
+            for g in range(PASSES):
+                copy(
+                    out=grouped[:, g].rearrange("p (n i) t -> p n t i", i=RUN),
+                    in_=raw[c][:, g].rearrange("p t (n i) -> p n t i", i=RUN),
+                )
+            x_codes.append(code_pool.tile([P, PASSES, CHUNK], U32, align_bytes=64, name="x_codes"))
+            x_scales.append(code_pool.tile([P, PASSES, CHUNK], U8, align_bytes=64, name="x_scales"))
+            nc.vector.quantize_mx(
+                out=x_codes[c][:].rearrange("p g n -> p (g n)").bitcast(FP8X4),
+                scales=x_scales[c][:].rearrange("p g n -> p (g n)"),
+                in_=grouped[:].rearrange("p g n t -> p (g n t)"),
+            )
+
+        def convolve_and_pool(c, m):
+            acc = acc_pool.tile([P, CHUNK], F32)
+            o_cols = slice(m * P, (m + 1) * P)
+            for g in range(PASSES):
+                nc.tensor.matmul_mx(
+                    out=acc[:],
+                    lhsT=w_words[:, g, o_cols].bitcast(FP8X4),
+                    lhsT_scale=w_planes[:, g, o_cols],
+                    rhs=x_codes[c][:, g, :].bitcast(FP8X4),
+                    rhs_scale=x_scales[c][:, g, :],
+                    start=(g == 0),
+                    stop=(g == PASSES - 1),
+                )
+            nc.vector.tensor_reduce(
+                out=pooled[:, m, c * WINDOWS : (c + 1) * WINDOWS].rearrange(
+                    "p (i j) -> p i j", j=POOLED_COLS
+                ),
+                in_=acc[:].rearrange(
+                    "p (i di j dj) -> p i j di dj", di=POOL, j=POOLED_COLS, dj=POOL
+                ),
+                axis=mybir.AxisListType.XY,
+                op=mybir.AluOpType.max,
+            )
+
+        def convolve_chunk(c):
+            for m in range(O_TILES):
+                if m == STAGE_AT and c + 1 < CHUNKS:
+                    stage_chunk(c + 1, nc.scalar.copy)
+                convolve_and_pool(c, m)
+
+        stage_chunk(0, nc.vector.tensor_copy)
+        convolve_chunk(0)
+
+        nc.scalar.copy(out=bias_rows_f32[:], in_=bias_rows[:])
+        bias_flip = flip_pool.tile([P, P], F32, tag="flip")
+        nc.tensor.transpose(bias_flip[:], bias_rows_f32[:], identity[:])
+        nc.scalar.copy(out=bias_cols[:], in_=bias_flip[:, 0:O_TILES])
+
+        for c in range(1, CHUNKS):
+            convolve_chunk(c)
+
+        def add_bias(m):
+            nc.scalar.activation(
+                out=result[:, m, :],
+                in_=pooled[:, m, :],
+                func=mybir.ActivationFunctionType.Identity,
+                bias=bias_cols[:, m : m + 1],
+            )
+
+        for m in range(V_TILES):
+            add_bias(m)
+            nc.sync.dma_start(out=out_v[0, m * P : (m + 1) * P, :], in_=result[:, m, :])
+        add_bias(Q_TILE)
+        add_bias(K_TILE)
+        nc.sync.dma_start(out=out_k[0], in_=result[:, K_TILE, :])
+        q_flip = flip_pool.tile([P, POSITIONS // P, P], F32, tag="flip")
+        for h in range(POSITIONS // P):
+            nc.tensor.transpose(q_flip[:, h, :], result[:, Q_TILE, h * P : (h + 1) * P], identity[:])
+        nc.scalar.copy(out=q_flipped[:], in_=q_flip[:])
+        nc.sync.dma_start(out=out_q[0].rearrange("(h n) o -> n h o", n=P), in_=q_flipped[:])

@@ -14,7 +14,7 @@ P = 128
 PACK = 4
 CHANNELS = 1024
 PASSES = CHANNELS // (P * PACK)
-QUADRANTS = 4
+QUADRANT = 32
 LIVE_ROWS = 4
 
 WIDTH = 64
@@ -22,9 +22,8 @@ POOL = 4
 PIXELS = WIDTH * WIDTH
 CHUNK = 512
 CHUNKS = PIXELS // CHUNK
-POOLED_ROWS = CHUNK // (WIDTH * POOL)
 POOLED_COLS = WIDTH // POOL
-WINDOWS = POOLED_ROWS * POOLED_COLS
+WINDOWS = CHUNK // (POOL * POOL)
 POSITIONS = PIXELS // (POOL * POOL)
 
 V_OUT = 1024
@@ -36,7 +35,7 @@ O_ALL = O_TILES * P
 
 RUN = 4
 ACC_BANKS = 7
-STAGE_AT = 7
+STAGE_AT = 5
 
 FLOPS = 2 * O_ALL * CHANNELS * PIXELS
 
@@ -70,20 +69,17 @@ def tile_selfattentionpatch_pa_t_kernel(
         make_identity(nc, identity[:])
 
         x_rows = x.rearrange("b (g p t) h w -> (b g) p t (h w)", p=P, t=PACK)
-        raw = []
+        raw = [raw_pool.tile([P, PASSES, PACK, CHUNK], BF16, name="raw") for c in range(CHUNKS)]
 
-        def load_chunk(c):
-            raw.append(raw_pool.tile([P, PASSES, PACK, CHUNK], BF16, name="raw"))
-            for g in range(PASSES):
-                nc.sync.dma_start(
-                    out=raw[c][:, g], in_=x_rows[g, :, :, c * CHUNK : (c + 1) * CHUNK]
-                )
+        def load_x(c, g):
+            nc.sync.dma_start(out=raw[c][:, g], in_=x_rows[g, :, :, c * CHUNK : (c + 1) * CHUNK])
 
         def load_scales(scales, first, count):
             rows = scales.rearrange("g (q r) o -> q r g o", r=LIVE_ROWS)
-            for q in range(QUADRANTS):
+            for q in range(P // QUADRANT):
+                live = slice(QUADRANT * q, QUADRANT * q + LIVE_ROWS)
                 nc.sync.dma_start(
-                    out=w_planes[32 * q : 32 * q + LIVE_ROWS, :, first : first + count].bitcast(I32),
+                    out=w_planes[live, :, first : first + count].bitcast(I32),
                     in_=rows[q].bitcast(I32),
                 )
 
@@ -94,20 +90,22 @@ def tile_selfattentionpatch_pa_t_kernel(
                 in_=view[:, :, PACK * begin : PACK * end].bitcast(I32),
             )
 
-        load_chunk(0)
+        for g in range(PASSES):
+            load_x(0, g)
         load_scales(wv_scales, 0, V_OUT)
-        load_words(wv_words, 0, 0, V_OUT // 2)
-        load_words(wv_words, 0, V_OUT // 2, V_OUT)
-        nc.scalar.dma_start(out=bias_rows[0:V_TILES, :], in_=bv.rearrange("(r o) -> r o", o=P))
-        nc.scalar.dma_start(out=bias_rows[Q_TILE : Q_TILE + 1, :], in_=bq.rearrange("(r o) -> r o", o=P))
-        nc.scalar.dma_start(out=bias_rows[K_TILE : K_TILE + 1, :], in_=bk.rearrange("(r o) -> r o", o=P))
-        load_chunk(1)
+        for g in range(PASSES):
+            load_x(1, g)
+            load_words(wv_words, 0, g * V_OUT // 2, (g + 1) * V_OUT // 2)
+        for c in range(2, CHUNKS):
+            for g in range(PASSES):
+                load_x(c, g)
+        nc.sync.dma_start(out=bias_rows[0:V_TILES, :], in_=bv.rearrange("(r o) -> r o", o=P))
+        nc.sync.dma_start(out=bias_rows[Q_TILE : Q_TILE + 1, :], in_=bq.rearrange("(r o) -> r o", o=P))
+        nc.sync.dma_start(out=bias_rows[K_TILE : K_TILE + 1, :], in_=bk.rearrange("(r o) -> r o", o=P))
         load_scales(wq_scales, Q_TILE * P, P)
         load_words(wq_words, Q_TILE * P, 0, P)
         load_scales(wk_scales, K_TILE * P, P)
         load_words(wk_words, K_TILE * P, 0, P)
-        for c in range(2, CHUNKS):
-            load_chunk(c)
 
         x_codes = []
         x_scales = []
@@ -151,23 +149,6 @@ def tile_selfattentionpatch_pa_t_kernel(
                 op=mybir.AluOpType.max,
             )
 
-        def convolve_chunk(c):
-            for m in range(O_TILES):
-                if m == STAGE_AT and c + 1 < CHUNKS:
-                    stage_chunk(c + 1, nc.scalar.copy)
-                convolve_and_pool(c, m)
-
-        stage_chunk(0, nc.vector.tensor_copy)
-        convolve_chunk(0)
-
-        nc.scalar.copy(out=bias_rows_f32[:], in_=bias_rows[:])
-        bias_flip = flip_pool.tile([P, P], F32, tag="flip")
-        nc.tensor.transpose(bias_flip[:], bias_rows_f32[:], identity[:])
-        nc.scalar.copy(out=bias_cols[:], in_=bias_flip[:, 0:O_TILES])
-
-        for c in range(1, CHUNKS):
-            convolve_chunk(c)
-
         def add_bias(m):
             nc.scalar.activation(
                 out=result[:, m, :],
@@ -176,14 +157,31 @@ def tile_selfattentionpatch_pa_t_kernel(
                 bias=bias_cols[:, m : m + 1],
             )
 
+        stage_chunk(0, nc.vector.tensor_copy)
+        for c in range(CHUNKS):
+            for m in range(V_TILES):
+                if m == STAGE_AT and c + 1 < CHUNKS:
+                    stage_chunk(c + 1, nc.scalar.copy)
+                convolve_and_pool(c, m)
+
+        nc.scalar.copy(out=bias_rows_f32[:], in_=bias_rows[:])
+        bias_flip = flip_pool.tile([P, P], F32, tag="flip")
+        nc.tensor.transpose(bias_flip[:], bias_rows_f32[:], identity[:])
+        nc.scalar.copy(out=bias_cols[:], in_=bias_flip[:, 0:O_TILES])
+
         for m in range(V_TILES):
             add_bias(m)
             nc.sync.dma_start(out=out_v[0, m * P : (m + 1) * P, :], in_=result[:, m, :])
+
+        for c in range(CHUNKS):
+            convolve_and_pool(c, Q_TILE)
         add_bias(Q_TILE)
-        add_bias(K_TILE)
-        nc.sync.dma_start(out=out_k[0], in_=result[:, K_TILE, :])
+        for c in range(CHUNKS):
+            convolve_and_pool(c, K_TILE)
         q_flip = flip_pool.tile([P, POSITIONS // P, P], F32, tag="flip")
         for h in range(POSITIONS // P):
             nc.tensor.transpose(q_flip[:, h, :], result[:, Q_TILE, h * P : (h + 1) * P], identity[:])
         nc.scalar.copy(out=q_flipped[:], in_=q_flip[:])
         nc.sync.dma_start(out=out_q[0].rearrange("(h n) o -> n h o", n=P), in_=q_flipped[:])
+        add_bias(K_TILE)
+        nc.sync.dma_start(out=out_k[0], in_=result[:, K_TILE, :])

@@ -107,6 +107,18 @@ def tile_selfattentionpatch_pa_t_kernel(
         load_scales(wk_scales, K_TILE * P, P)
         load_words(wk_words, K_TILE * P, 0, P)
 
+        warm = flip_pool.tile([P, CHUNK], F32, tag="flip", name="warm")
+
+        def keep_warm(c, g, count):
+            for i in range(count):
+                nc.tensor.matmul(
+                    out=warm[:], lhsT=raw[c][:, g, 0, 0:P], rhs=raw[c][:, g, i % PACK, :], start=True, stop=True
+                )
+
+        keep_warm(0, 0, 3)
+        keep_warm(0, 1, 3)
+        keep_warm(1, 0, 4)
+
         x_codes = []
         x_scales = []
 

@@ -36,6 +36,10 @@ O_ALL = O_TILES * P
 RUN = 4
 ACC_BANKS = 7
 STAGE_AT = 5
+G_BANKS = 6
+LAG = 2
+SIDE_AT = 3
+HUGE = 3.0e38
 
 FLOPS = 2 * O_ALL * CHANNELS * PIXELS
 
@@ -52,6 +56,7 @@ def tile_selfattentionpatch_pa_t_kernel(
         code_pool = ctx.enter_context(tc.tile_pool(name="codes", bufs=CHUNKS))
         acc_pool = ctx.enter_context(tc.psum_pool(name="acc", bufs=ACC_BANKS))
         flip_pool = ctx.enter_context(tc.psum_pool(name="flip", bufs=1))
+        tree_pool = ctx.enter_context(tc.tile_pool(name="tree", bufs=2))
         ctx.enter_context(tc.manual_schedule())
 
         w_words = keep.tile([P, PASSES, O_ALL], U32, align_bytes=64)
@@ -99,11 +104,12 @@ def tile_selfattentionpatch_pa_t_kernel(
         for c in range(2, CHUNKS):
             for g in range(PASSES):
                 load_x(c, g)
+            if c == 3:
+                load_scales(wq_scales, Q_TILE * P, P)
+                load_words(wq_words, Q_TILE * P, 0, P)
         nc.sync.dma_start(out=bias_rows[0:V_TILES, :], in_=bv.rearrange("(r o) -> r o", o=P))
         nc.sync.dma_start(out=bias_rows[Q_TILE : Q_TILE + 1, :], in_=bq.rearrange("(r o) -> r o", o=P))
         nc.sync.dma_start(out=bias_rows[K_TILE : K_TILE + 1, :], in_=bk.rearrange("(r o) -> r o", o=P))
-        load_scales(wq_scales, Q_TILE * P, P)
-        load_words(wq_words, Q_TILE * P, 0, P)
         load_scales(wk_scales, K_TILE * P, P)
         load_words(wk_words, K_TILE * P, 0, P)
 
@@ -122,13 +128,19 @@ def tile_selfattentionpatch_pa_t_kernel(
         x_codes = []
         x_scales = []
 
-        def stage_chunk(c, copy):
+        grouped_of = {}
+
+        def regroup(c, copy):
             grouped = grouped_pool.tile([P, PASSES, CHUNK, PACK], BF16, align_bytes=64)
             for g in range(PASSES):
                 copy(
                     out=grouped[:, g].rearrange("p (n i) t -> p n t i", i=RUN),
                     in_=raw[c][:, g].rearrange("p t (n i) -> p n t i", i=RUN),
                 )
+            grouped_of[c] = grouped
+
+        def quantise(c):
+            grouped = grouped_of[c]
             x_codes.append(code_pool.tile([P, PASSES, CHUNK], U32, align_bytes=64, name="x_codes"))
             x_scales.append(code_pool.tile([P, PASSES, CHUNK], U8, align_bytes=64, name="x_scales"))
             nc.vector.quantize_mx(
@@ -137,8 +149,7 @@ def tile_selfattentionpatch_pa_t_kernel(
                 in_=grouped[:].rearrange("p g n t -> p (g n t)"),
             )
 
-        def convolve_and_pool(c, m):
-            acc = acc_pool.tile([P, CHUNK], F32)
+        def convolve(acc, c, m):
             o_cols = slice(m * P, (m + 1) * P)
             for g in range(PASSES):
                 nc.tensor.matmul_mx(
@@ -150,12 +161,50 @@ def tile_selfattentionpatch_pa_t_kernel(
                     start=(g == 0),
                     stop=(g == PASSES - 1),
                 )
+
+        def convolve_and_pool(c, m):
+            acc = acc_pool.tile([P, CHUNK], F32)
+            convolve(acc, c, m)
             nc.vector.tensor_reduce(
                 out=pooled[:, m, c * WINDOWS : (c + 1) * WINDOWS].rearrange(
                     "p (i j) -> p i j", j=POOLED_COLS
                 ),
                 in_=acc[:].rearrange(
                     "p (i di j dj) -> p i j di dj", di=POOL, j=POOLED_COLS, dj=POOL
+                ),
+                axis=mybir.AxisListType.XY,
+                op=mybir.AluOpType.max,
+            )
+
+        side_of = {}
+        half_of = {}
+
+        def convolve_beside(c):
+            side_of[c] = flip_pool.tile([P, CHUNK], F32, tag="flip", name="side")
+            convolve(side_of[c], c, Q_TILE)
+
+        def halve_beside(c):
+            spill = tree_pool.tile([P, CHUNK], F32)
+            nc.scalar.copy(out=spill[:], in_=side_of[c][:])
+            rows = spill[:].rearrange("p (i h r) -> p i h r", i=2, h=2)
+            upper = rows[:, :, 0, :]
+            lower = rows[:, :, 1, :]
+            diff = tree_pool.tile([P, 2, CHUNK // 4], F32)
+            half_of[c] = tree_pool.tile([P, 2, CHUNK // 4], F32, name="half")
+            nc.gpsimd.tensor_tensor(out=diff[:], in0=upper, in1=lower, op=mybir.AluOpType.subtract)
+            nc.gpsimd.tensor_scalar(
+                out=diff[:], in0=diff[:], scalar1=HUGE, scalar2=0.0,
+                op0=mybir.AluOpType.min, op1=mybir.AluOpType.max,
+            )
+            nc.gpsimd.tensor_tensor(out=half_of[c][:], in0=diff[:], in1=lower, op=mybir.AluOpType.add)
+
+        def finish(c):
+            nc.vector.tensor_reduce(
+                out=pooled[:, Q_TILE, c * WINDOWS : (c + 1) * WINDOWS].rearrange(
+                    "p (i j) -> p i j", j=POOLED_COLS
+                ),
+                in_=half_of[c][:].rearrange(
+                    "p i (di j dj) -> p i j di dj", di=POOL // 2, j=POOLED_COLS, dj=POOL
                 ),
                 axis=mybir.AxisListType.XY,
                 op=mybir.AluOpType.max,
@@ -169,11 +218,21 @@ def tile_selfattentionpatch_pa_t_kernel(
                 bias=bias_cols[:, m : m + 1],
             )
 
-        stage_chunk(0, nc.vector.tensor_copy)
+        regroup(0, nc.vector.tensor_copy)
+        quantise(0)
         for c in range(CHUNKS):
             for m in range(V_TILES):
-                if m == STAGE_AT and c + 1 < CHUNKS:
-                    stage_chunk(c + 1, nc.scalar.copy)
+                if m == SIDE_AT and 0 <= c - LAG < G_BANKS:
+                    convolve_beside(c - LAG)
+                if m == STAGE_AT:
+                    if c + 1 < CHUNKS:
+                        regroup(c + 1, nc.scalar.copy)
+                    if 0 <= c - LAG < G_BANKS:
+                        halve_beside(c - LAG)
+                    if c + 1 < CHUNKS:
+                        quantise(c + 1)
+                    if 0 <= c - LAG - 1 < G_BANKS:
+                        finish(c - LAG - 1)
                 convolve_and_pool(c, m)
 
         nc.scalar.copy(out=bias_rows_f32[:], in_=bias_rows[:])
@@ -185,8 +244,9 @@ def tile_selfattentionpatch_pa_t_kernel(
             add_bias(m)
             nc.sync.dma_start(out=out_v[0, m * P : (m + 1) * P, :], in_=result[:, m, :])
 
-        for c in range(CHUNKS):
+        for c in range(G_BANKS, CHUNKS):
             convolve_and_pool(c, Q_TILE)
+        finish(G_BANKS - 1)
         add_bias(Q_TILE)
         for c in range(CHUNKS):
             convolve_and_pool(c, K_TILE)

@@ -39,6 +39,7 @@ STAGE_AT = 5
 G_BANKS = 6
 LAG = 2
 SIDE_AT = 3
+V_SHARE = 352
 HUGE = 3.0e38
 
 FLOPS = 2 * O_ALL * CHANNELS * PIXELS
@@ -123,19 +124,19 @@ def tile_selfattentionpatch_pa_t_kernel(
 
         keep_warm(0, 0, 3)
         keep_warm(0, 1, 3)
-        keep_warm(1, 0, 4)
+        keep_warm(1, 0, 2)
 
         x_codes = []
         x_scales = []
 
         grouped_of = {}
 
-        def regroup(c, copy):
+        def regroup(c, shares):
             grouped = grouped_pool.tile([P, PASSES, CHUNK, PACK], BF16, align_bytes=64)
-            for g in range(PASSES):
+            for g, begin, end, copy in shares:
                 copy(
-                    out=grouped[:, g].rearrange("p (n i) t -> p n t i", i=RUN),
-                    in_=raw[c][:, g].rearrange("p t (n i) -> p n t i", i=RUN),
+                    out=grouped[:, g, begin:end, :].rearrange("p (n i) t -> p n t i", i=RUN),
+                    in_=raw[c][:, g, :, begin:end].rearrange("p t (n i) -> p n t i", i=RUN),
                 )
             grouped_of[c] = grouped
 
@@ -218,7 +219,12 @@ def tile_selfattentionpatch_pa_t_kernel(
                 bias=bias_cols[:, m : m + 1],
             )
 
-        regroup(0, nc.vector.tensor_copy)
+        by_scalar = [(g, 0, CHUNK, nc.scalar.copy) for g in range(PASSES)]
+        regroup(0, (
+            (0, 0, CHUNK, nc.vector.tensor_copy),
+            (1, 0, V_SHARE, nc.vector.tensor_copy),
+            (1, V_SHARE, CHUNK, nc.scalar.copy),
+        ))
         quantise(0)
         for c in range(CHUNKS):
             for m in range(V_TILES):
@@ -226,7 +232,7 @@ def tile_selfattentionpatch_pa_t_kernel(
                     convolve_beside(c - LAG)
                 if m == STAGE_AT:
                     if c + 1 < CHUNKS:
-                        regroup(c + 1, nc.scalar.copy)
+                        regroup(c + 1, by_scalar)
                     if 0 <= c - LAG < G_BANKS:
                         halve_beside(c - LAG)
                     if c + 1 < CHUNKS:

from contextlib import ExitStack

import concourse.mybir as mybir
from concourse.masks import make_identity

F32 = mybir.dt.float32
BF16 = mybir.dt.bfloat16
I32 = mybir.dt.int32
U32 = mybir.dt.uint32
U8 = mybir.dt.uint8
FP8X4 = mybir.dt.float8_e4m3fn_x4

P = 128
PACK = 4
CHANNELS = 1024
PASSES = CHANNELS // (P * PACK)
QUADRANT = 32
LIVE_ROWS = 4

WIDTH = 64
POOL = 4
PIXELS = WIDTH * WIDTH
CHUNK = 512
CHUNKS = PIXELS // CHUNK
POOLED_COLS = WIDTH // POOL
WINDOWS = CHUNK // (POOL * POOL)
POSITIONS = PIXELS // (POOL * POOL)

V_OUT = 1024
V_TILES = V_OUT // P
Q_TILE = V_TILES
K_TILE = V_TILES + 1
O_TILES = V_TILES + 2
O_ALL = O_TILES * P

RUN = 4
ACC_BANKS = 7
STAGE_AT = 5
G_BANKS = 6
LAG = 2
SIDE_AT = 3
V_SHARE = 352
HUGE = 3.0e38

FLOPS = 2 * O_ALL * CHANNELS * PIXELS


def tile_selfattentionpatch_pa_t_kernel(
    tc, x, wq_words, wq_scales, bq, wk_words, wk_scales, bk, wv_words, wv_scales, bv,
    out_q, out_k, out_v,
):
    nc = tc.nc
    with ExitStack() as ctx:
        keep = ctx.enter_context(tc.tile_pool(name="keep", bufs=1))
        raw_pool = ctx.enter_context(tc.tile_pool(name="raw", bufs=CHUNKS))
        grouped_pool = ctx.enter_context(tc.tile_pool(name="grouped", bufs=3))
        code_pool = ctx.enter_context(tc.tile_pool(name="codes", bufs=CHUNKS))
        acc_pool = ctx.enter_context(tc.psum_pool(name="acc", bufs=ACC_BANKS))
        flip_pool = ctx.enter_context(tc.psum_pool(name="flip", bufs=1))
        tree_pool = ctx.enter_context(tc.tile_pool(name="tree", bufs=2))
        ctx.enter_context(tc.manual_schedule())

        w_words = keep.tile([P, PASSES, O_ALL], U32, align_bytes=64)
        w_planes = keep.tile([P, PASSES, O_ALL], U8, align_bytes=64)
        bias_rows = keep.tile([P, P], BF16)
        bias_rows_f32 = keep.tile([P, P], F32)
        bias_cols = keep.tile([P, O_TILES], F32)
        identity = keep.tile([P, P], F32)
        pooled = keep.tile([P, O_TILES, POSITIONS], F32)
        result = keep.tile([P, O_TILES, POSITIONS], F32)
        q_flipped = keep.tile([P, POSITIONS // P, P], F32)

        nc.vector.memset(w_planes[:].rearrange("p g o -> p (g o)").bitcast(I32), 0)
        nc.vector.memset(bias_rows[:].bitcast(I32), 0)
        make_identity(nc, identity[:])

        x_rows = x.rearrange("b (g p t) h w -> (b g) p t (h w)", p=P, t=PACK)
        raw = [raw_pool.tile([P, PASSES, PACK, CHUNK], BF16, name="raw") for c in range(CHUNKS)]

        def load_x(c, g):
            nc.sync.dma_start(out=raw[c][:, g], in_=x_rows[g, :, :, c * CHUNK : (c + 1) * CHUNK])

        def load_scales(scales, first, count):
            rows = scales.rearrange("g (q r) o -> q r g o", r=LIVE_ROWS)
            for q in range(P // QUADRANT):
                live = slice(QUADRANT * q, QUADRANT * q + LIVE_ROWS)
                nc.sync.dma_start(
                    out=w_planes[live, :, first : first + count].bitcast(I32),
                    in_=rows[q].bitcast(I32),
                )

        def load_words(words, first, begin, end):
            view = words.rearrange("g p o t -> p g (o t)")
            nc.sync.dma_start(
                out=w_words[:, :, first + begin : first + end].bitcast(I32),
                in_=view[:, :, PACK * begin : PACK * end].bitcast(I32),
            )

        for g in range(PASSES):
            load_x(0, g)
        load_scales(wv_scales, 0, V_OUT)
        for g in range(PASSES):
            load_x(1, g)
            load_words(wv_words, 0, g * V_OUT // 2, (g + 1) * V_OUT // 2)
        for c in range(2, CHUNKS):
            for g in range(PASSES):
                load_x(c, g)
            if c == 3:
                load_scales(wq_scales, Q_TILE * P, P)
                load_words(wq_words, Q_TILE * P, 0, P)
        nc.sync.dma_start(out=bias_rows[0:V_TILES, :], in_=bv.rearrange("(r o) -> r o", o=P))
        nc.sync.dma_start(out=bias_rows[Q_TILE : Q_TILE + 1, :], in_=bq.rearrange("(r o) -> r o", o=P))
        nc.sync.dma_start(out=bias_rows[K_TILE : K_TILE + 1, :], in_=bk.rearrange("(r o) -> r o", o=P))
        load_scales(wk_scales, K_TILE * P, P)
        load_words(wk_words, K_TILE * P, 0, P)

        warm = flip_pool.tile([P, CHUNK], F32, tag="flip", name="warm")

        def keep_warm(c, g, count):
            for i in range(count):
                nc.tensor.matmul(
                    out=warm[:], lhsT=raw[c][:, g, 0, 0:P], rhs=raw[c][:, g, i % PACK, :], start=True, stop=True
                )

        keep_warm(0, 0, 3)
        keep_warm(0, 1, 3)
        keep_warm(1, 0, 2)

        x_codes = []
        x_scales = []

        grouped_of = {}

        def regroup(c, shares):
            grouped = grouped_pool.tile([P, PASSES, CHUNK, PACK], BF16, align_bytes=64)
            for g, begin, end, copy in shares:
                copy(
                    out=grouped[:, g, begin:end, :].rearrange("p (n i) t -> p n t i", i=RUN),
                    in_=raw[c][:, g, :, begin:end].rearrange("p t (n i) -> p n t i", i=RUN),
                )
            grouped_of[c] = grouped

        def quantise(c):
            grouped = grouped_of[c]
            x_codes.append(code_pool.tile([P, PASSES, CHUNK], U32, align_bytes=64, name="x_codes"))
            x_scales.append(code_pool.tile([P, PASSES, CHUNK], U8, align_bytes=64, name="x_scales"))
            nc.vector.quantize_mx(
                out=x_codes[c][:].rearrange("p g n -> p (g n)").bitcast(FP8X4),
                scales=x_scales[c][:].rearrange("p g n -> p (g n)"),
                in_=grouped[:].rearrange("p g n t -> p (g n t)"),
            )

        def convolve(acc, c, m):
            o_cols = slice(m * P, (m + 1) * P)
            for g in range(PASSES):
                nc.tensor.matmul_mx(
                    out=acc[:],
                    lhsT=w_words[:, g, o_cols].bitcast(FP8X4),
                    lhsT_scale=w_planes[:, g, o_cols],
                    rhs=x_codes[c][:, g, :].bitcast(FP8X4),
                    rhs_scale=x_scales[c][:, g, :],
                    start=(g == 0),
                    stop=(g == PASSES - 1),
                )

        def convolve_and_pool(c, m):
            acc = acc_pool.tile([P, CHUNK], F32)
            convolve(acc, c, m)
            nc.vector.tensor_reduce(
                out=pooled[:, m, c * WINDOWS : (c + 1) * WINDOWS].rearrange(
                    "p (i j) -> p i j", j=POOLED_COLS
                ),
                in_=acc[:].rearrange(
                    "p (i di j dj) -> p i j di dj", di=POOL, j=POOLED_COLS, dj=POOL
                ),
                axis=mybir.AxisListType.XY,
                op=mybir.AluOpType.max,
            )

        side_of = {}
        half_of = {}

        def convolve_beside(c):
            side_of[c] = flip_pool.tile([P, CHUNK], F32, tag="flip", name="side")
            convolve(side_of[c], c, Q_TILE)

        def halve_beside(c):
            spill = tree_pool.tile([P, CHUNK], F32)
            nc.scalar.copy(out=spill[:], in_=side_of[c][:])
            rows = spill[:].rearrange("p (i h r) -> p i h r", i=2, h=2)
            upper = rows[:, :, 0, :]
            lower = rows[:, :, 1, :]
            diff = tree_pool.tile([P, 2, CHUNK // 4], F32)
            half_of[c] = tree_pool.tile([P, 2, CHUNK // 4], F32, name="half")
            nc.gpsimd.tensor_tensor(out=diff[:], in0=upper, in1=lower, op=mybir.AluOpType.subtract)
            nc.gpsimd.tensor_scalar(
                out=diff[:], in0=diff[:], scalar1=HUGE, scalar2=0.0,
                op0=mybir.AluOpType.min, op1=mybir.AluOpType.max,
            )
            nc.gpsimd.tensor_tensor(out=half_of[c][:], in0=diff[:], in1=lower, op=mybir.AluOpType.add)

        def finish(c):
            nc.vector.tensor_reduce(
                out=pooled[:, Q_TILE, c * WINDOWS : (c + 1) * WINDOWS].rearrange(
                    "p (i j) -> p i j", j=POOLED_COLS
                ),
                in_=half_of[c][:].rearrange(
                    "p i (di j dj) -> p i j di dj", di=POOL // 2, j=POOLED_COLS, dj=POOL
                ),
                axis=mybir.AxisListType.XY,
                op=mybir.AluOpType.max,
            )

        def add_bias(m):
            nc.scalar.activation(
                out=result[:, m, :],
                in_=pooled[:, m, :],
                func=mybir.ActivationFunctionType.Identity,
                bias=bias_cols[:, m : m + 1],
            )

        by_scalar = [(g, 0, CHUNK, nc.scalar.copy) for g in range(PASSES)]
        regroup(0, (
            (0, 0, CHUNK, nc.vector.tensor_copy),
            (1, 0, V_SHARE, nc.vector.tensor_copy),
            (1, V_SHARE, CHUNK, nc.scalar.copy),
        ))
        quantise(0)
        for c in range(CHUNKS):
            for m in range(V_TILES):
                if m == SIDE_AT and 0 <= c - LAG < G_BANKS:
                    convolve_beside(c - LAG)
                if m == STAGE_AT:
                    if c + 1 < CHUNKS:
                        regroup(c + 1, by_scalar)
                    if 0 <= c - LAG < G_BANKS:
                        halve_beside(c - LAG)
                    if c + 1 < CHUNKS:
                        quantise(c + 1)
                    if 0 <= c - LAG - 1 < G_BANKS:
                        finish(c - LAG - 1)
                convolve_and_pool(c, m)

        nc.scalar.copy(out=bias_rows_f32[:], in_=bias_rows[:])
        bias_flip = flip_pool.tile([P, P], F32, tag="flip")
        nc.tensor.transpose(bias_flip[:], bias_rows_f32[:], identity[:])
        nc.scalar.copy(out=bias_cols[:], in_=bias_flip[:, 0:O_TILES])

        for m in range(V_TILES):
            add_bias(m)
            nc.sync.dma_start(out=out_v[0, m * P : (m + 1) * P, :], in_=result[:, m, :])

        for c in range(G_BANKS, CHUNKS):
            convolve_and_pool(c, Q_TILE)
        finish(G_BANKS - 1)
        add_bias(Q_TILE)
        for c in range(CHUNKS):
            convolve_and_pool(c, K_TILE)
        q_flip = flip_pool.tile([P, POSITIONS // P, P], F32, tag="flip")
        for h in range(POSITIONS // P):
            nc.tensor.transpose(q_flip[:, h, :], result[:, Q_TILE, h * P : (h + 1) * P], identity[:])
        nc.scalar.copy(out=q_flipped[:], in_=q_flip[:])
        nc.sync.dma_start(out=out_q[0].rearrange("(h n) o -> n h o", n=P), in_=q_flipped[:])
        add_bias(K_TILE)
        nc.sync.dma_start(out=out_k[0], in_=result[:, K_TILE, :])
